import numpy as np
import ml_dtypes


def mxq(x, axis, fmt="e4m3"):
    dtype, down = {"e4m3": (ml_dtypes.float8_e4m3fn, 7), "e5m2": (ml_dtypes.float8_e5m2, 14)}[fmt]
    v = np.moveaxis(np.asarray(x, np.float32).astype(ml_dtypes.bfloat16).astype(np.float64), axis, -1)
    blocks = v.reshape(v.shape[:-1] + (-1, 32))
    amax = np.abs(blocks).max(-1, keepdims=True)
    byte = np.maximum(np.where(amax > 0, np.frexp(amax)[1] - 1 + 127, 0) - down, 1)
    scale = np.exp2(byte - 127.0)
    codes = (blocks / scale).astype(np.float32).astype(dtype).astype(np.float64)
    return np.moveaxis((codes * scale).reshape(v.shape), -1, axis)


WIDE = False


def mx_kscale(k):
    if not WIDE:
        return np.ones(k)
    levels = np.array([10, -10, 5, -5, 0])
    if k % 512:
        return np.exp2(np.random.permutation(np.resize(levels, k // 32))).repeat(32)
    a = np.empty((k // 512, 16))
    for p in range(k // 512):
        a[p, :8] = np.random.permutation(np.resize(levels, 8))
        for g in range(8):
            far = levels[np.abs(levels - a[p, g]) >= 10]
            a[p, g + 8] = far[np.random.randint(len(far))]
    return np.exp2(a.ravel()).repeat(32)


BF16 = ml_dtypes.bfloat16


def bf(x):
    return np.asarray(x, np.float32).astype(BF16)


def f64(x):
    return np.asarray(x).astype(np.float64)


B, N, K, H, C_E, M = 2, 256, 32, 256, 1024, 512
SCALE = 30.0


def setup_inputs():
    s = mx_kscale(M)
    return {"h2": bf(np.random.standard_normal((B, N, K, M)) * 0.65 * s),
            "h_V": bf(np.random.standard_normal((B, N, H))),
            "mask_attend": bf(np.random.uniform(size=(B, N, K)) < 0.9),
            "W3_w": bf(np.random.standard_normal((M, H)) * 4.0 / np.sqrt(M) / s[:, None]),
            "W3_b": bf(np.random.standard_normal(H) * 0.1)}


def reference(h2, h_V, mask_attend, W3_w, W3_b):
    h_message = (mxq(f64(h2), 3, "e4m3") @ mxq(f64(W3_w), 0, "e4m3")) + f64(W3_b)
    h_message = f64(mask_attend)[..., None] * h_message
    dh = np.sum(h_message, axis=-2) / SCALE
    return f64(h_V) + dh

@@ -1,0 +1,199 @@
+from contextlib import ExitStack
+
+import concourse.masks as masks
+import concourse.mybir as mybir
+
+F32 = mybir.dt.float32
+BF16 = mybir.dt.bfloat16
+U32 = mybir.dt.uint32
+U8 = mybir.dt.uint8
+FP8X4 = mybir.dt.float8_e4m3fn_x4
+MULT = mybir.AluOpType.mult
+ADD = mybir.AluOpType.add
+
+P = 128
+PACK = 4
+NODES = 2 * 256
+EDGES = 32
+M = 512
+H = 256
+SCALE = 30.0
+
+NODE_TILES = NODES // P
+WORDS = M // 2
+HALVES = WORDS // P
+GROUP = 4
+GROUPS_PER_TILE = EDGES // GROUP
+N_GROUPS = NODE_TILES * GROUPS_PER_TILE
+BANK_EDGES = 2
+GROUPS_PER_RUN = 4
+N_RUNS = N_GROUPS // GROUPS_PER_RUN
+LAG = 2
+
+FLOPS = 2 * NODES * EDGES * M * H
+
+
+def tile_declayerj_pb_t_kernel(tc, h2, h_V, mask_attend, W3_w, W3_b, out):
+    nc = tc.nc
+    h2_nodes = h2.rearrange("b n k m -> (b n) (k m)").rearrange("(p i) f -> p i f", p=P)
+    mask_nodes = mask_attend.rearrange("b n k -> (b n) k").rearrange("(p i) k -> p i k", p=P)
+    hv_nodes = h_V.rearrange("b n h -> (b n) h").rearrange("(p i) h -> p i h", p=P)
+    out_nodes = out.rearrange("b n h -> (b n) h").rearrange("(p i) h -> p i h", p=P)
+
+    with ExitStack() as ctx:
+        const = ctx.enter_context(tc.tile_pool(name="const", bufs=1))
+        x_pool = ctx.enter_context(tc.tile_pool(name="x", bufs=N_GROUPS))
+        sel_pool = ctx.enter_context(tc.tile_pool(name="sel", bufs=2 * GROUPS_PER_RUN))
+        grouped_pool = ctx.enter_context(tc.tile_pool(name="grouped", bufs=GROUPS_PER_RUN + LAG))
+        mx_pool = ctx.enter_context(tc.tile_pool(name="mx", bufs=2 * GROUPS_PER_RUN))
+        tail = ctx.enter_context(tc.tile_pool(name="tail", bufs=2))
+        xt_pool = ctx.enter_context(tc.psum_pool(name="xt", bufs=6))
+        acc_pool = ctx.enter_context(tc.psum_pool(name="acc", bufs=2))
+        ctx.enter_context(tc.manual_schedule())
+
+        ident = const.tile([P, P], F32)
+        masks.make_identity(nc, ident[:])
+        ones = const.tile([P, P], BF16)
+        nc.vector.memset(ones[:], 1.0)
+        bias_rows = const.tile([P, H], BF16)
+        nc.vector.memset(bias_rows[:], 0.0)
+
+        mask_bf = const.tile([P, NODE_TILES, EDGES], BF16)
+        nc.sync.dma_start(out=mask_bf[:], in_=mask_nodes)
+        nc.sync.dma_start(out=bias_rows[0:1, :], in_=W3_b.unsqueeze(0))
+        w_raw = const.tile([P, PACK, H], BF16)
+        hv = const.tile([P, NODE_TILES, H], BF16)
+        x_of = {}
+        for g in range(N_GROUPS):
+            i, q = divmod(g, GROUPS_PER_TILE)
+            x_of[g] = x_pool.tile([P, GROUP * M], BF16, name="x")
+            nc.sync.dma_start(
+                out=x_of[g][:],
+                in_=h2_nodes[:, i, q * GROUP * M : (q + 1) * GROUP * M],
+            )
+            if g == 0:
+                nc.sync.dma_start(
+                    out=w_raw[:],
+                    in_=W3_w.rearrange("(p t) h -> p t h", p=P),
+                )
+            if g == GROUPS_PER_TILE - 1:
+                nc.sync.dma_start(out=hv[:], in_=hv_nodes)
+
+        bias_ps = acc_pool.tile([P, H], F32, name="bias_ps", tag="acc")
+        nc.tensor.matmul(out=bias_ps[:], lhsT=ones[:], rhs=bias_rows[:], start=True, stop=True)
+        bias_all = const.tile([P, H], F32)
+        nc.scalar.copy(out=bias_all[:], in_=bias_ps[:])
+
+        mask_f32 = const.tile([P, NODE_TILES, EDGES], F32)
+        nc.vector.tensor_copy(out=mask_f32[:], in_=mask_bf[:])
+        count = const.tile([P, NODE_TILES], F32)
+        nc.vector.reduce_sum(out=count[:], in_=mask_f32[:], axis=mybir.AxisListType.X)
+        count_scaled = const.tile([P, NODE_TILES], F32)
+        nc.vector.tensor_scalar_mul(out=count_scaled[:], in0=count[:], scalar1=1.0 / SCALE)
+
+        sel_of = {}
+        grouped_of = {}
+        codes_of = {}
+        scales_of = {}
+        acc_of = {}
+
+        def build_selectors(g):
+            i, q = divmod(g, GROUPS_PER_TILE)
+            sel_of[g] = sel_pool.tile([P, GROUP, P], F32, name="sel")
+            for j in range(GROUP):
+                k = q * GROUP + j
+                nc.vector.tensor_scalar_mul(
+                    out=sel_of[g][:, j, :], in0=ident[:], scalar1=mask_f32[:, i, k : k + 1]
+                )
+
+        def transpose_group(g):
+            x_words = x_of[g][:].bitcast(F32)
+            grouped_of[g] = grouped_pool.tile(
+                [P, GROUP * P * PACK], BF16, name="grouped", align_bytes=64
+            )
+            grouped_words = grouped_of[g][:].bitcast(F32)
+            bank_words = BANK_EDGES * P * HALVES
+            for b in range(GROUP // BANK_EDGES):
+                xt = xt_pool.tile([P, BANK_EDGES, HALVES, P], F32, name="xt")
+                for jj in range(BANK_EDGES):
+                    j = b * BANK_EDGES + jj
+                    for u in range(HALVES):
+                        nc.tensor.transpose(
+                            xt[:, jj, u, :],
+                            x_words[:, j * WORDS + u : (j + 1) * WORDS : HALVES],
+                            sel_of[g][:, j, :],
+                        )
+                nc.scalar.copy(
+                    out=grouped_words[:, b * bank_words : (b + 1) * bank_words].rearrange(
+                        "p (j n u) -> p j n u", j=BANK_EDGES, u=HALVES
+                    ),
+                    in_=xt[:].rearrange("p j u n -> p j n u"),
+                )
+
+        def quantise_group(g):
+            codes_of[g] = mx_pool.tile([P, GROUP * P], U32, name="codes", align_bytes=64)
+            scales_of[g] = mx_pool.tile([P, GROUP * P], U8, name="scales", align_bytes=64)
+            nc.vector.quantize_mx(
+                out=codes_of[g][:].bitcast(FP8X4), scales=scales_of[g][:], in_=grouped_of[g][:]
+            )
+
+        def multiply_group(g):
+            i, q = divmod(g, GROUPS_PER_TILE)
+            if q == 0:
+                acc_of[i] = acc_pool.tile([P, H], F32, name="acc", tag="acc")
+            for j in range(GROUP):
+                k = q * GROUP + j
+                nodes = slice(j * P, (j + 1) * P)
+                nc.tensor.matmul_mx(
+                    out=acc_of[i][:],
+                    lhsT=codes_of[g][:, nodes].bitcast(FP8X4),
+                    lhsT_scale=scales_of[g][:, nodes],
+                    rhs=w_codes[:].bitcast(FP8X4),
+                    rhs_scale=w_scales[:],
+                    start=(k == 0),
+                    stop=(k == EDGES - 1),
+                )
+            if q == GROUPS_PER_TILE - 1:
+                finish_node_tile(i)
+
+        def finish_node_tile(i):
+            rest = tail.tile([P, H], F32, name="rest")
+            nc.vector.scalar_tensor_tensor(
+                out=rest[:],
+                in0=bias_all[:],
+                scalar=count_scaled[:, i : i + 1],
+                in1=hv[:, i, :],
+                op0=MULT,
+                op1=ADD,
+            )
+            result = tail.tile([P, H], F32, name="result")
+            nc.vector.scalar_tensor_tensor(
+                out=result[:], in0=acc_of[i][:], scalar=1.0 / SCALE, in1=rest[:], op0=MULT, op1=ADD
+            )
+            nc.sync.dma_start(out=out_nodes[:, i, :], in_=result[:])
+
+        def groups_of_run(r):
+            return range(r * GROUPS_PER_RUN, min((r + 1) * GROUPS_PER_RUN, N_GROUPS))
+
+        for g in groups_of_run(0):
+            build_selectors(g)
+        w_grouped = const.tile([P, H, PACK], BF16, align_bytes=64)
+        nc.vector.tensor_copy(out=w_grouped[:], in_=w_raw[:].rearrange("p t h -> p h t"))
+        w_codes = const.tile([P, H], U32, align_bytes=64)
+        w_scales = const.tile([P, H], U8, align_bytes=64)
+        nc.vector.quantize_mx(
+            out=w_codes[:].bitcast(FP8X4),
+            scales=w_scales[:],
+            in_=w_grouped[:].rearrange("p h t -> p (h t)"),
+        )
+
+        for r in range(N_RUNS + 1):
+            for g in groups_of_run(r):
+                transpose_group(g)
+            for g in groups_of_run(r + 1):
+                build_selectors(g)
+            for g in groups_of_run(r):
+                quantise_group(g)
+            first = max(r * GROUPS_PER_RUN - LAG, 0)
+            for g in range(first, min((r + 1) * GROUPS_PER_RUN - LAG, N_GROUPS)):
+                multiply_group(g)

@@ -1,7 +1,7 @@
 from contextlib import ExitStack
 
-import concourse.masks as masks
 import concourse.mybir as mybir
+import concourse.masks as masks
 
 F32 = mybir.dt.float32
 BF16 = mybir.dt.bfloat16
@@ -20,14 +20,16 @@ H = 256
 SCALE = 30.0
 
 NODE_TILES = NODES // P
+BLOCKS = M // 32
+HALF = 16
+HALVES = 2
 WORDS = M // 2
-HALVES = WORDS // P
 GROUP = 4
 GROUPS_PER_TILE = EDGES // GROUP
 N_GROUPS = NODE_TILES * GROUPS_PER_TILE
 BANK_EDGES = 2
-GROUPS_PER_RUN = 4
-N_RUNS = N_GROUPS // GROUPS_PER_RUN
+LOADS = [1, 1, 2] + [4] * 30 + [2, 1, 1]
+RUNS = [1, 1, 2] + [4] * 6 + [2, 1, 1]
 LAG = 2
 
 FLOPS = 2 * NODES * EDGES * M * H
@@ -42,10 +44,10 @@ def tile_declayerj_pb_t_kernel(tc, h2, h_V, mask_attend, W3_w, W3_b, out):
 
     with ExitStack() as ctx:
         const = ctx.enter_context(tc.tile_pool(name="const", bufs=1))
-        x_pool = ctx.enter_context(tc.tile_pool(name="x", bufs=N_GROUPS))
-        sel_pool = ctx.enter_context(tc.tile_pool(name="sel", bufs=2 * GROUPS_PER_RUN))
-        grouped_pool = ctx.enter_context(tc.tile_pool(name="grouped", bufs=GROUPS_PER_RUN + LAG))
-        mx_pool = ctx.enter_context(tc.tile_pool(name="mx", bufs=2 * GROUPS_PER_RUN))
+        x_pool = ctx.enter_context(tc.tile_pool(name="x", bufs=1))
+        perm_pool = ctx.enter_context(tc.tile_pool(name="perm", bufs=8))
+        grouped_pool = ctx.enter_context(tc.tile_pool(name="grouped", bufs=4))
+        mx_pool = ctx.enter_context(tc.tile_pool(name="mx", bufs=8))
         tail = ctx.enter_context(tc.tile_pool(name="tail", bufs=2))
         xt_pool = ctx.enter_context(tc.psum_pool(name="xt", bufs=6))
         acc_pool = ctx.enter_context(tc.psum_pool(name="acc", bufs=2))
@@ -60,54 +62,52 @@ def tile_declayerj_pb_t_kernel(tc, h2, h_V, mask_attend, W3_w, W3_b, out):
 
         mask_bf = const.tile([P, NODE_TILES, EDGES], BF16)
         nc.sync.dma_start(out=mask_bf[:], in_=mask_nodes)
-        nc.sync.dma_start(out=bias_rows[0:1, :], in_=W3_b.unsqueeze(0))
-        w_raw = const.tile([P, PACK, H], BF16)
+        w_raw = const.tile([P, HALVES, 2 * H], BF16)
         hv = const.tile([P, NODE_TILES, H], BF16)
         x_of = {}
-        for g in range(N_GROUPS):
-            i, q = divmod(g, GROUPS_PER_TILE)
-            x_of[g] = x_pool.tile([P, GROUP * M], BF16, name="x")
-            nc.sync.dma_start(
-                out=x_of[g][:],
-                in_=h2_nodes[:, i, q * GROUP * M : (q + 1) * GROUP * M],
-            )
-            if g == 0:
-                nc.sync.dma_start(
-                    out=w_raw[:],
-                    in_=W3_w.rearrange("(p t) h -> p t h", p=P),
-                )
-            if g == GROUPS_PER_TILE - 1:
+        edge = 0
+        for n, edges in enumerate(LOADS):
+            i, k = divmod(edge, EDGES)
+            x = x_pool.tile([P, edges * M], BF16, name="x%d" % n)
+            nc.sync.dma_start(out=x[:], in_=h2_nodes[:, i, k * M : (k + edges) * M])
+            for j in range(edges):
+                x_of[edge + j] = (x, j * M)
+            edge += edges
+            if n == 1:
+                w_rows = W3_w.rearrange("(q u j e) h -> u q j (e h)", q=BLOCKS, u=HALVES, e=2)
+                for u in range(HALVES):
+                    nc.sync.dma_start(out=w_raw[:, u, :], in_=w_rows[u])
+                nc.sync.dma_start(out=bias_rows[0:1, :], in_=W3_b.unsqueeze(0))
+            if n == 8:
                 nc.sync.dma_start(out=hv[:], in_=hv_nodes)
-
-        bias_ps = acc_pool.tile([P, H], F32, name="bias_ps", tag="acc")
-        nc.tensor.matmul(out=bias_ps[:], lhsT=ones[:], rhs=bias_rows[:], start=True, stop=True)
-        bias_all = const.tile([P, H], F32)
-        nc.scalar.copy(out=bias_all[:], in_=bias_ps[:])
 
         mask_f32 = const.tile([P, NODE_TILES, EDGES], F32)
         nc.vector.tensor_copy(out=mask_f32[:], in_=mask_bf[:])
-        count = const.tile([P, NODE_TILES], F32)
-        nc.vector.reduce_sum(out=count[:], in_=mask_f32[:], axis=mybir.AxisListType.X)
-        count_scaled = const.tile([P, NODE_TILES], F32)
-        nc.vector.tensor_scalar_mul(out=count_scaled[:], in0=count[:], scalar1=1.0 / SCALE)
 
-        sel_of = {}
+        perm_of = {}
         grouped_of = {}
         codes_of = {}
         scales_of = {}
         acc_of = {}
+        rest_of = {}
 
-        def build_selectors(g):
-            i, q = divmod(g, GROUPS_PER_TILE)
-            sel_of[g] = sel_pool.tile([P, GROUP, P], F32, name="sel")
+        def permute_group(g):
+            perm_of[g] = perm_pool.tile([P, GROUP * M], BF16, name="perm")
             for j in range(GROUP):
-                k = q * GROUP + j
+                i, k = divmod(g * GROUP + j, EDGES)
+                x, first = x_of[g * GROUP + j]
                 nc.vector.tensor_scalar_mul(
-                    out=sel_of[g][:, j, :], in0=ident[:], scalar1=mask_f32[:, i, k : k + 1]
+                    out=perm_of[g][:, j * M : (j + 1) * M].rearrange(
+                        "p (u q c) -> p u q c", u=HALVES, c=HALF
+                    ),
+                    in0=x[:, first : first + M].rearrange(
+                        "p (q u c) -> p u q c", u=HALVES, c=HALF
+                    ),
+                    scalar1=mask_f32[:, i, k : k + 1],
                 )
 
         def transpose_group(g):
-            x_words = x_of[g][:].bitcast(F32)
+            words = perm_of[g][:].bitcast(F32)
             grouped_of[g] = grouped_pool.tile(
                 [P, GROUP * P * PACK], BF16, name="grouped", align_bytes=64
             )
@@ -116,12 +116,10 @@ def tile_declayerj_pb_t_kernel(tc, h2, h_V, mask_attend, W3_w, W3_b, out):
             for b in range(GROUP // BANK_EDGES):
                 xt = xt_pool.tile([P, BANK_EDGES, HALVES, P], F32, name="xt")
                 for jj in range(BANK_EDGES):
-                    j = b * BANK_EDGES + jj
                     for u in range(HALVES):
+                        first = (b * BANK_EDGES + jj) * WORDS + u * P
                         nc.tensor.transpose(
-                            xt[:, jj, u, :],
-                            x_words[:, j * WORDS + u : (j + 1) * WORDS : HALVES],
-                            sel_of[g][:, j, :],
+                            xt[:, jj, u, :], words[:, first : first + P], ident[:]
                         )
                 nc.scalar.copy(
                     out=grouped_words[:, b * bank_words : (b + 1) * bank_words].rearrange(
@@ -153,47 +151,84 @@ def tile_declayerj_pb_t_kernel(tc, h2, h_V, mask_attend, W3_w, W3_b, out):
                     start=(k == 0),
                     stop=(k == EDGES - 1),
                 )
-            if q == GROUPS_PER_TILE - 1:
-                finish_node_tile(i)
 
-        def finish_node_tile(i):
-            rest = tail.tile([P, H], F32, name="rest")
+        def prepare_rest(i):
+            rest_of[i] = const.tile([P, H], F32, name="rest%d" % i)
             nc.vector.scalar_tensor_tensor(
-                out=rest[:],
+                out=rest_of[i][:],
                 in0=bias_all[:],
                 scalar=count_scaled[:, i : i + 1],
                 in1=hv[:, i, :],
                 op0=MULT,
                 op1=ADD,
             )
+
+        def finish_node_tile(i):
             result = tail.tile([P, H], F32, name="result")
             nc.vector.scalar_tensor_tensor(
-                out=result[:], in0=acc_of[i][:], scalar=1.0 / SCALE, in1=rest[:], op0=MULT, op1=ADD
+                out=result[:],
+                in0=acc_of[i][:],
+                scalar=1.0 / SCALE,
+                in1=rest_of[i][:],
+                op0=MULT,
+                op1=ADD,
             )
             nc.sync.dma_start(out=out_nodes[:, i, :], in_=result[:])
 
-        def groups_of_run(r):
-            return range(r * GROUPS_PER_RUN, min((r + 1) * GROUPS_PER_RUN, N_GROUPS))
+        run_groups = []
+        g = 0
+        for size in RUNS:
+            run_groups.append(list(range(g, g + size)))
+            g += size
 
-        for g in groups_of_run(0):
-            build_selectors(g)
+        permute_group(0)
+        transpose_group(0)
+        permute_group(1)
         w_grouped = const.tile([P, H, PACK], BF16, align_bytes=64)
-        nc.vector.tensor_copy(out=w_grouped[:], in_=w_raw[:].rearrange("p t h -> p h t"))
+        nc.scalar.copy(
+            out=w_grouped[:].rearrange("p h (u e) -> p h u e", u=HALVES),
+            in_=w_raw[:].rearrange("p u (e h) -> p h u e", e=2),
+        )
         w_codes = const.tile([P, H], U32, align_bytes=64)
         w_scales = const.tile([P, H], U8, align_bytes=64)
+        quantise_group(0)
         nc.vector.quantize_mx(
             out=w_codes[:].bitcast(FP8X4),
             scales=w_scales[:],
             in_=w_grouped[:].rearrange("p h t -> p (h t)"),
         )
+        bias_ps = acc_pool.tile([P, H], F32, name="bias_ps", tag="acc")
+        nc.tensor.matmul(out=bias_ps[:], lhsT=ones[:], rhs=bias_rows[:], start=True, stop=True)
+        bias_all = const.tile([P, H], F32)
+        nc.scalar.copy(out=bias_all[:], in_=bias_ps[:])
+        count = const.tile([P, NODE_TILES], F32)
+        nc.vector.reduce_sum(out=count[:], in_=mask_f32[:], axis=mybir.AxisListType.X)
+        count_scaled = const.tile([P, NODE_TILES], F32)
+        nc.vector.tensor_scalar_mul(out=count_scaled[:], in0=count[:], scalar1=1.0 / SCALE)
 
-        for r in range(N_RUNS + 1):
-            for g in groups_of_run(r):
+        multiplied = 0
+        unfinished = []
+        for r in range(1, len(run_groups) + 1):
+            now = run_groups[r] if r < len(run_groups) else []
+            after = run_groups[r + 1] if r + 1 < len(run_groups) else []
+            for g in now:
                 transpose_group(g)
-            for g in groups_of_run(r + 1):
-                build_selectors(g)
-            for g in groups_of_run(r):
-                quantise_group(g)
-            first = max(r * GROUPS_PER_RUN - LAG, 0)
-            for g in range(first, min((r + 1) * GROUPS_PER_RUN - LAG, N_GROUPS)):
-                multiply_group(g)
+            ready = now[-1] + 1 - LAG if now else N_GROUPS
+            for n in range(max(len(now), len(after))):
+                if n < len(after):
+                    permute_group(after[n])
+                if n < len(now):
+                    quantise_group(now[n])
+            for i in unfinished:
+                finish_node_tile(i)
+            unfinished = []
+            if r == 4:
+                for i in range(NODE_TILES):
+                    prepare_rest(i)
+            while multiplied < ready:
+                multiply_group(multiplied)
+                multiplied += 1
+                if multiplied % GROUPS_PER_TILE == 0:
+                    unfinished.append(multiplied // GROUPS_PER_TILE - 1)
+        for i in unfinished:
+            finish_node_tile(i)

@@ -29,8 +29,8 @@ GROUPS_PER_TILE = EDGES // GROUP
 N_GROUPS = NODE_TILES * GROUPS_PER_TILE
 BANK_EDGES = 2
 LOADS = [1, 1, 2] + [4] * 30 + [2, 1, 1]
-RUNS = [1, 1, 2] + [4] * 6 + [2, 1, 1]
-LAG = 2
+RUNS = [1, 1, 2, 3] + [4] * 5 + [3, 1, 1]
+LAG = 3
 
 FLOPS = 2 * NODES * EDGES * M * H
 
@@ -73,16 +73,13 @@ def tile_declayerj_pb_t_kernel(tc, h2, h_V, mask_attend, W3_w, W3_b, out):
             for j in range(edges):
                 x_of[edge + j] = (x, j * M)
             edge += edges
-            if n == 1:
+            if n == 3:
                 w_rows = W3_w.rearrange("(q u j e) h -> u q j (e h)", q=BLOCKS, u=HALVES, e=2)
                 for u in range(HALVES):
                     nc.sync.dma_start(out=w_raw[:, u, :], in_=w_rows[u])
                 nc.sync.dma_start(out=bias_rows[0:1, :], in_=W3_b.unsqueeze(0))
             if n == 8:
                 nc.sync.dma_start(out=hv[:], in_=hv_nodes)
-
-        mask_f32 = const.tile([P, NODE_TILES, EDGES], F32)
-        nc.vector.tensor_copy(out=mask_f32[:], in_=mask_bf[:])
 
         perm_of = {}
         grouped_of = {}
@@ -103,7 +100,7 @@ def tile_declayerj_pb_t_kernel(tc, h2, h_V, mask_attend, W3_w, W3_b, out):
                     in0=x[:, first : first + M].rearrange(
                         "p (q u c) -> p u q c", u=HALVES, c=HALF
                     ),
-                    scalar1=mask_f32[:, i, k : k + 1],
+                    scalar1=mask_bf[:, i, k : k + 1],
                 )
 
         def transpose_group(g):
@@ -181,34 +178,37 @@ def tile_declayerj_pb_t_kernel(tc, h2, h_V, mask_attend, W3_w, W3_b, out):
             run_groups.append(list(range(g, g + size)))
             g += size
 
-        permute_group(0)
-        transpose_group(0)
-        permute_group(1)
         w_grouped = const.tile([P, H, PACK], BF16, align_bytes=64)
-        nc.scalar.copy(
-            out=w_grouped[:].rearrange("p h (u e) -> p h u e", u=HALVES),
-            in_=w_raw[:].rearrange("p u (e h) -> p h u e", e=2),
-        )
         w_codes = const.tile([P, H], U32, align_bytes=64)
         w_scales = const.tile([P, H], U8, align_bytes=64)
-        quantise_group(0)
-        nc.vector.quantize_mx(
-            out=w_codes[:].bitcast(FP8X4),
-            scales=w_scales[:],
-            in_=w_grouped[:].rearrange("p h t -> p (h t)"),
-        )
-        bias_ps = acc_pool.tile([P, H], F32, name="bias_ps", tag="acc")
-        nc.tensor.matmul(out=bias_ps[:], lhsT=ones[:], rhs=bias_rows[:], start=True, stop=True)
         bias_all = const.tile([P, H], F32)
-        nc.scalar.copy(out=bias_all[:], in_=bias_ps[:])
         count = const.tile([P, NODE_TILES], F32)
-        nc.vector.reduce_sum(out=count[:], in_=mask_f32[:], axis=mybir.AxisListType.X)
         count_scaled = const.tile([P, NODE_TILES], F32)
-        nc.vector.tensor_scalar_mul(out=count_scaled[:], in0=count[:], scalar1=1.0 / SCALE)
+
+        def prepare_weights():
+            nc.vector.tensor_copy(
+                out=w_grouped[:].rearrange("p h (u e) -> p h u e", u=HALVES),
+                in_=w_raw[:].rearrange("p u (e h) -> p h u e", e=2),
+            )
+            nc.vector.reduce_sum(out=count[:], in_=mask_bf[:], axis=mybir.AxisListType.X)
+            nc.vector.quantize_mx(
+                out=w_codes[:].bitcast(FP8X4),
+                scales=w_scales[:],
+                in_=w_grouped[:].rearrange("p h t -> p (h t)"),
+            )
+            nc.vector.tensor_scalar_mul(out=count_scaled[:], in0=count[:], scalar1=1.0 / SCALE)
+            bias_ps = acc_pool.tile([P, H], F32, name="bias_ps", tag="acc")
+            nc.tensor.matmul(
+                out=bias_ps[:], lhsT=ones[:], rhs=bias_rows[:], start=True, stop=True
+            )
+            nc.scalar.copy(out=bias_all[:], in_=bias_ps[:])
+
+        for g in run_groups[0]:
+            permute_group(g)
 
         multiplied = 0
         unfinished = []
-        for r in range(1, len(run_groups) + 1):
+        for r in range(len(run_groups) + 1):
             now = run_groups[r] if r < len(run_groups) else []
             after = run_groups[r + 1] if r + 1 < len(run_groups) else []
             for g in now:
@@ -219,6 +219,8 @@ def tile_declayerj_pb_t_kernel(tc, h2, h_V, mask_attend, W3_w, W3_b, out):
                     permute_group(after[n])
                 if n < len(now):
                     quantise_group(now[n])
+            if r == 0:
+                prepare_weights()
             for i in unfinished:
                 finish_node_tile(i)
             unfinished = []

@@ -29,7 +29,7 @@ GROUPS_PER_TILE = EDGES // GROUP
 N_GROUPS = NODE_TILES * GROUPS_PER_TILE
 BANK_EDGES = 2
 LOADS = [1, 1, 2] + [4] * 30 + [2, 1, 1]
-RUNS = [1, 1, 2, 3] + [4] * 5 + [3, 1, 1]
+RUNS = [1, 1] + [3] * 10
 LAG = 3
 
 FLOPS = 2 * NODES * EDGES * M * H

@@ -81,6 +81,9 @@ def tile_declayerj_pb_t_kernel(tc, h2, h_V, mask_attend, W3_w, W3_b, out):
             if n == 8:
                 nc.sync.dma_start(out=hv[:], in_=hv_nodes)
 
+        mask_f32 = const.tile([P, NODE_TILES, EDGES], F32)
+        nc.vector.tensor_copy(out=mask_f32[:], in_=mask_bf[:])
+
         perm_of = {}
         grouped_of = {}
         codes_of = {}
@@ -88,19 +91,29 @@ def tile_declayerj_pb_t_kernel(tc, h2, h_V, mask_attend, W3_w, W3_b, out):
         acc_of = {}
         rest_of = {}
 
+        def permute_edge(out, in_, mask):
+            out = out.rearrange("p (u q c) -> p u q c", u=HALVES, c=HALF)
+            in_ = in_.rearrange("p (q u c) -> p u q c", u=HALVES, c=HALF)
+            nc.vector.tensor_scalar_mul(out=out, in0=in_, scalar1=mask)
+
+        def permute_edge_scalar(out, in_, mask):
+            out = out.rearrange("p (u q c) -> p u q c", u=HALVES, c=HALF)
+            in_ = in_.rearrange("p (q u c) -> p u q c", u=HALVES, c=HALF)
+            nc.scalar.activation(
+                out=out, in_=in_, func=mybir.ActivationFunctionType.Copy, scale=mask
+            )
+
         def permute_group(g):
             perm_of[g] = perm_pool.tile([P, GROUP * M], BF16, name="perm")
             for j in range(GROUP):
                 i, k = divmod(g * GROUP + j, EDGES)
                 x, first = x_of[g * GROUP + j]
-                nc.vector.tensor_scalar_mul(
-                    out=perm_of[g][:, j * M : (j + 1) * M].rearrange(
-                        "p (u q c) -> p u q c", u=HALVES, c=HALF
-                    ),
-                    in0=x[:, first : first + M].rearrange(
-                        "p (q u c) -> p u q c", u=HALVES, c=HALF
-                    ),
-                    scalar1=mask_bf[:, i, k : k + 1],
+                last = j == GROUP - 1 and g >= 4 and g % 3 == 1
+                permute = permute_edge_scalar if last else permute_edge
+                permute(
+                    perm_of[g][:, j * M : (j + 1) * M],
+                    x[:, first : first + M],
+                    mask_f32[:, i, k : k + 1],
                 )
 
         def transpose_group(g):
@@ -185,11 +198,13 @@ def tile_declayerj_pb_t_kernel(tc, h2, h_V, mask_attend, W3_w, W3_b, out):
         count = const.tile([P, NODE_TILES], F32)
         count_scaled = const.tile([P, NODE_TILES], F32)
 
-        def prepare_weights():
-            nc.vector.tensor_copy(
+        def interleave_weights():
+            nc.scalar.copy(
                 out=w_grouped[:].rearrange("p h (u e) -> p h u e", u=HALVES),
                 in_=w_raw[:].rearrange("p u (e h) -> p h u e", e=2),
             )
+
+        def prepare_weights():
             nc.vector.reduce_sum(out=count[:], in_=mask_bf[:], axis=mybir.AxisListType.X)
             nc.vector.quantize_mx(
                 out=w_codes[:].bitcast(FP8X4),
@@ -214,12 +229,14 @@ def tile_declayerj_pb_t_kernel(tc, h2, h_V, mask_attend, W3_w, W3_b, out):
             for g in now:
                 transpose_group(g)
             ready = now[-1] + 1 - LAG if now else N_GROUPS
+            if r == 1:
+                interleave_weights()
             for n in range(max(len(now), len(after))):
                 if n < len(after):
                     permute_group(after[n])
                 if n < len(now):
                     quantise_group(now[n])
-            if r == 0:
+            if r == 1:
                 prepare_weights()
             for i in unfinished:
                 finish_node_tile(i)

@@ -108,7 +108,7 @@ def tile_declayerj_pb_t_kernel(tc, h2, h_V, mask_attend, W3_w, W3_b, out):
             for j in range(GROUP):
                 i, k = divmod(g * GROUP + j, EDGES)
                 x, first = x_of[g * GROUP + j]
-                last = j == GROUP - 1 and g >= 4 and g % 3 == 1
+                last = j == GROUP - 1 and 4 <= g < 29 and g % 3 == 1
                 permute = permute_edge_scalar if last else permute_edge
                 permute(
                     perm_of[g][:, j * M : (j + 1) * M],
@@ -131,7 +131,8 @@ def tile_declayerj_pb_t_kernel(tc, h2, h_V, mask_attend, W3_w, W3_b, out):
                         nc.tensor.transpose(
                             xt[:, jj, u, :], words[:, first : first + P], ident[:]
                         )
-                nc.scalar.copy(
+                copy = nc.vector.tensor_copy if g == run_groups[-1][0] and b == 1 else nc.scalar.copy
+                copy(
                     out=grouped_words[:, b * bank_words : (b + 1) * bank_words].rearrange(
                         "p (j n u) -> p j n u", j=BANK_EDGES, u=HALVES
                     ),
@@ -231,6 +232,11 @@ def tile_declayerj_pb_t_kernel(tc, h2, h_V, mask_attend, W3_w, W3_b, out):
             ready = now[-1] + 1 - LAG if now else N_GROUPS
             if r == 1:
                 interleave_weights()
+            if not after:
+                for i in unfinished:
+                    finish_node_tile(i)
+                    prepare_rest(i + 1)
+                unfinished = []
             for n in range(max(len(now), len(after))):
                 if n < len(after):
                     permute_group(after[n])
@@ -242,7 +248,7 @@ def tile_declayerj_pb_t_kernel(tc, h2, h_V, mask_attend, W3_w, W3_b, out):
                 finish_node_tile(i)
             unfinished = []
             if r == 4:
-                for i in range(NODE_TILES):
+                for i in range(NODE_TILES - 1):
                     prepare_rest(i)
             while multiplied < ready:
                 multiply_group(multiplied)

from contextlib import ExitStack

import concourse.mybir as mybir
import concourse.masks as masks

F32 = mybir.dt.float32
BF16 = mybir.dt.bfloat16
U32 = mybir.dt.uint32
U8 = mybir.dt.uint8
FP8X4 = mybir.dt.float8_e4m3fn_x4
MULT = mybir.AluOpType.mult
ADD = mybir.AluOpType.add

P = 128
PACK = 4
NODES = 2 * 256
EDGES = 32
M = 512
H = 256
SCALE = 30.0

NODE_TILES = NODES // P
BLOCKS = M // 32
HALF = 16
HALVES = 2
WORDS = M // 2
GROUP = 4
GROUPS_PER_TILE = EDGES // GROUP
N_GROUPS = NODE_TILES * GROUPS_PER_TILE
BANK_EDGES = 2
LOADS = [1, 1, 2] + [4] * 30 + [2, 1, 1]
RUNS = [1, 1] + [3] * 10
LAG = 3

FLOPS = 2 * NODES * EDGES * M * H


def tile_declayerj_pb_t_kernel(tc, h2, h_V, mask_attend, W3_w, W3_b, out):
    nc = tc.nc
    h2_nodes = h2.rearrange("b n k m -> (b n) (k m)").rearrange("(p i) f -> p i f", p=P)
    mask_nodes = mask_attend.rearrange("b n k -> (b n) k").rearrange("(p i) k -> p i k", p=P)
    hv_nodes = h_V.rearrange("b n h -> (b n) h").rearrange("(p i) h -> p i h", p=P)
    out_nodes = out.rearrange("b n h -> (b n) h").rearrange("(p i) h -> p i h", p=P)

    with ExitStack() as ctx:
        const = ctx.enter_context(tc.tile_pool(name="const", bufs=1))
        x_pool = ctx.enter_context(tc.tile_pool(name="x", bufs=1))
        perm_pool = ctx.enter_context(tc.tile_pool(name="perm", bufs=8))
        grouped_pool = ctx.enter_context(tc.tile_pool(name="grouped", bufs=4))
        mx_pool = ctx.enter_context(tc.tile_pool(name="mx", bufs=8))
        tail = ctx.enter_context(tc.tile_pool(name="tail", bufs=2))
        xt_pool = ctx.enter_context(tc.psum_pool(name="xt", bufs=6))
        acc_pool = ctx.enter_context(tc.psum_pool(name="acc", bufs=2))
        ctx.enter_context(tc.manual_schedule())

        ident = const.tile([P, P], F32)
        masks.make_identity(nc, ident[:])
        ones = const.tile([P, P], BF16)
        nc.vector.memset(ones[:], 1.0)
        bias_rows = const.tile([P, H], BF16)
        nc.vector.memset(bias_rows[:], 0.0)

        mask_bf = const.tile([P, NODE_TILES, EDGES], BF16)
        nc.sync.dma_start(out=mask_bf[:], in_=mask_nodes)
        w_raw = const.tile([P, HALVES, 2 * H], BF16)
        hv = const.tile([P, NODE_TILES, H], BF16)
        x_of = {}
        edge = 0
        for n, edges in enumerate(LOADS):
            i, k = divmod(edge, EDGES)
            x = x_pool.tile([P, edges * M], BF16, name="x%d" % n)
            nc.sync.dma_start(out=x[:], in_=h2_nodes[:, i, k * M : (k + edges) * M])
            for j in range(edges):
                x_of[edge + j] = (x, j * M)
            edge += edges
            if n == 3:
                w_rows = W3_w.rearrange("(q u j e) h -> u q j (e h)", q=BLOCKS, u=HALVES, e=2)
                for u in range(HALVES):
                    nc.sync.dma_start(out=w_raw[:, u, :], in_=w_rows[u])
                nc.sync.dma_start(out=bias_rows[0:1, :], in_=W3_b.unsqueeze(0))
            if n == 8:
                nc.sync.dma_start(out=hv[:], in_=hv_nodes)

        mask_f32 = const.tile([P, NODE_TILES, EDGES], F32)
        nc.vector.tensor_copy(out=mask_f32[:], in_=mask_bf[:])

        perm_of = {}
        grouped_of = {}
        codes_of = {}
        scales_of = {}
        acc_of = {}
        rest_of = {}

        def permute_edge(out, in_, mask):
            out = out.rearrange("p (u q c) -> p u q c", u=HALVES, c=HALF)
            in_ = in_.rearrange("p (q u c) -> p u q c", u=HALVES, c=HALF)
            nc.vector.tensor_scalar_mul(out=out, in0=in_, scalar1=mask)

        def permute_edge_scalar(out, in_, mask):
            out = out.rearrange("p (u q c) -> p u q c", u=HALVES, c=HALF)
            in_ = in_.rearrange("p (q u c) -> p u q c", u=HALVES, c=HALF)
            nc.scalar.activation(
                out=out, in_=in_, func=mybir.ActivationFunctionType.Copy, scale=mask
            )

        def permute_group(g):
            perm_of[g] = perm_pool.tile([P, GROUP * M], BF16, name="perm")
            for j in range(GROUP):
                i, k = divmod(g * GROUP + j, EDGES)
                x, first = x_of[g * GROUP + j]
                last = j == GROUP - 1 and 4 <= g < 29 and g % 3 == 1
                permute = permute_edge_scalar if last else permute_edge
                permute(
                    perm_of[g][:, j * M : (j + 1) * M],
                    x[:, first : first + M],
                    mask_f32[:, i, k : k + 1],
                )

        def transpose_group(g):
            words = perm_of[g][:].bitcast(F32)
            grouped_of[g] = grouped_pool.tile(
                [P, GROUP * P * PACK], BF16, name="grouped", align_bytes=64
            )
            grouped_words = grouped_of[g][:].bitcast(F32)
            bank_words = BANK_EDGES * P * HALVES
            for b in range(GROUP // BANK_EDGES):
                xt = xt_pool.tile([P, BANK_EDGES, HALVES, P], F32, name="xt")
                for jj in range(BANK_EDGES):
                    for u in range(HALVES):
                        first = (b * BANK_EDGES + jj) * WORDS + u * P
                        nc.tensor.transpose(
                            xt[:, jj, u, :], words[:, first : first + P], ident[:]
                        )
                copy = nc.vector.tensor_copy if g == run_groups[-1][0] and b == 1 else nc.scalar.copy
                copy(
                    out=grouped_words[:, b * bank_words : (b + 1) * bank_words].rearrange(
                        "p (j n u) -> p j n u", j=BANK_EDGES, u=HALVES
                    ),
                    in_=xt[:].rearrange("p j u n -> p j n u"),
                )

        def quantise_group(g):
            codes_of[g] = mx_pool.tile([P, GROUP * P], U32, name="codes", align_bytes=64)
            scales_of[g] = mx_pool.tile([P, GROUP * P], U8, name="scales", align_bytes=64)
            nc.vector.quantize_mx(
                out=codes_of[g][:].bitcast(FP8X4), scales=scales_of[g][:], in_=grouped_of[g][:]
            )

        def multiply_group(g):
            i, q = divmod(g, GROUPS_PER_TILE)
            if q == 0:
                acc_of[i] = acc_pool.tile([P, H], F32, name="acc", tag="acc")
            for j in range(GROUP):
                k = q * GROUP + j
                nodes = slice(j * P, (j + 1) * P)
                nc.tensor.matmul_mx(
                    out=acc_of[i][:],
                    lhsT=codes_of[g][:, nodes].bitcast(FP8X4),
                    lhsT_scale=scales_of[g][:, nodes],
                    rhs=w_codes[:].bitcast(FP8X4),
                    rhs_scale=w_scales[:],
                    start=(k == 0),
                    stop=(k == EDGES - 1),
                )

        def prepare_rest(i):
            rest_of[i] = const.tile([P, H], F32, name="rest%d" % i)
            nc.vector.scalar_tensor_tensor(
                out=rest_of[i][:],
                in0=bias_all[:],
                scalar=count_scaled[:, i : i + 1],
                in1=hv[:, i, :],
                op0=MULT,
                op1=ADD,
            )

        def finish_node_tile(i):
            result = tail.tile([P, H], F32, name="result")
            nc.vector.scalar_tensor_tensor(
                out=result[:],
                in0=acc_of[i][:],
                scalar=1.0 / SCALE,
                in1=rest_of[i][:],
                op0=MULT,
                op1=ADD,
            )
            nc.sync.dma_start(out=out_nodes[:, i, :], in_=result[:])

        run_groups = []
        g = 0
        for size in RUNS:
            run_groups.append(list(range(g, g + size)))
            g += size

        w_grouped = const.tile([P, H, PACK], BF16, align_bytes=64)
        w_codes = const.tile([P, H], U32, align_bytes=64)
        w_scales = const.tile([P, H], U8, align_bytes=64)
        bias_all = const.tile([P, H], F32)
        count = const.tile([P, NODE_TILES], F32)
        count_scaled = const.tile([P, NODE_TILES], F32)

        def interleave_weights():
            nc.scalar.copy(
                out=w_grouped[:].rearrange("p h (u e) -> p h u e", u=HALVES),
                in_=w_raw[:].rearrange("p u (e h) -> p h u e", e=2),
            )

        def prepare_weights():
            nc.vector.reduce_sum(out=count[:], in_=mask_bf[:], axis=mybir.AxisListType.X)
            nc.vector.quantize_mx(
                out=w_codes[:].bitcast(FP8X4),
                scales=w_scales[:],
                in_=w_grouped[:].rearrange("p h t -> p (h t)"),
            )
            nc.vector.tensor_scalar_mul(out=count_scaled[:], in0=count[:], scalar1=1.0 / SCALE)
            bias_ps = acc_pool.tile([P, H], F32, name="bias_ps", tag="acc")
            nc.tensor.matmul(
                out=bias_ps[:], lhsT=ones[:], rhs=bias_rows[:], start=True, stop=True
            )
            nc.scalar.copy(out=bias_all[:], in_=bias_ps[:])

        for g in run_groups[0]:
            permute_group(g)

        multiplied = 0
        unfinished = []
        for r in range(len(run_groups) + 1):
            now = run_groups[r] if r < len(run_groups) else []
            after = run_groups[r + 1] if r + 1 < len(run_groups) else []
            for g in now:
                transpose_group(g)
            ready = now[-1] + 1 - LAG if now else N_GROUPS
            if r == 1:
                interleave_weights()
            if not after:
                for i in unfinished:
                    finish_node_tile(i)
                    prepare_rest(i + 1)
                unfinished = []
            for n in range(max(len(now), len(after))):
                if n < len(after):
                    permute_group(after[n])
                if n < len(now):
                    quantise_group(now[n])
            if r == 1:
                prepare_weights()
            for i in unfinished:
                finish_node_tile(i)
            unfinished = []
            if r == 4:
                for i in range(NODE_TILES - 1):
                    prepare_rest(i)
            while multiplied < ready:
                multiply_group(multiplied)
                multiplied += 1
                if multiplied % GROUPS_PER_TILE == 0:
                    unfinished.append(multiplied // GROUPS_PER_TILE - 1)
        for i in unfinished:
            finish_node_tile(i)
